import numpy as np
import ml_dtypes


def mxq(x, axis, fmt="e4m3"):
    dtype, down = {"e4m3": (ml_dtypes.float8_e4m3fn, 7), "e5m2": (ml_dtypes.float8_e5m2, 14)}[fmt]
    v = np.moveaxis(np.asarray(x, np.float32).astype(ml_dtypes.bfloat16).astype(np.float64), axis, -1)
    blocks = v.reshape(v.shape[:-1] + (-1, 32))
    amax = np.abs(blocks).max(-1, keepdims=True)
    byte = np.maximum(np.where(amax > 0, np.frexp(amax)[1] - 1 + 127, 0) - down, 1)
    scale = np.exp2(byte - 127.0)
    codes = (blocks / scale).astype(np.float32).astype(dtype).astype(np.float64)
    return np.moveaxis((codes * scale).reshape(v.shape), -1, axis)


WIDE = False


def mx_kscale(k):
    if not WIDE:
        return np.ones(k)
    levels = np.array([10, -10, 5, -5, 0])
    a = np.random.permutation(np.resize(levels, k // 512 * 4)).reshape(k // 512, 4)
    idx = np.arange(k)
    return np.exp2(a[idx // 512, idx % 128 // 32])


BF16 = ml_dtypes.bfloat16


def bf(x):
    return np.asarray(x, np.float32).astype(BF16)


def f64(x):
    return np.asarray(x).astype(np.float64)


E2M1 = np.array([0.0, 0.5, 1.0, 1.5, 2.0, 3.0, 4.0, 6.0, -0.0, -0.5, -1.0, -1.5, -2.0, -3.0, -4.0, -6.0])


def pack_weight(w, fmt):
    k, n = w.shape
    w = f64(bf(w)).reshape(k // 32, 32, n)
    amax = np.abs(w).max(1)
    if fmt == "e4m3":
        byte = np.frexp(amax)[1] - 1 + 127 - 7
    else:
        mant, ex = np.frexp(amax / 6.0)
        byte = np.where(mant > 0.5, ex, ex - 1) + 127
    byte = np.clip(np.where(amax > 0, byte, 1), 1, 254)
    scaled = (w * np.exp2(127.0 - byte)[:, None, :]).reshape(k, n).astype(np.float32)
    by_word = np.ascontiguousarray(scaled.reshape(k // 512, 128, 4, n).transpose(0, 1, 3, 2))
    if fmt == "e4m3":
        words = by_word.astype(ml_dtypes.float8_e4m3fn).view(np.uint8)
    else:
        c = by_word.astype(ml_dtypes.float4_e2m1fn).view(np.uint8) & 0xF
        words = c[..., 0::2] | (c[..., 1::2] << 4)
    return np.ascontiguousarray(words), np.ascontiguousarray(byte.astype(np.uint8).reshape(k // 512, 16, n))


def unpack_weight(words, scales, fmt):
    g, p, n, _ = words.shape
    if fmt == "e4m3":
        vals = np.ascontiguousarray(words).view(ml_dtypes.float8_e4m3fn).astype(np.float64)
    else:
        nib = np.empty((g, p, n, 4), np.uint8)
        nib[..., 0::2] = words & 0xF
        nib[..., 1::2] = words >> 4
        vals = E2M1[nib]
    vals = vals * np.repeat(np.exp2(scales.astype(np.float64) - 127.0), 8, axis=1)[..., None]
    return vals.transpose(0, 1, 3, 2).reshape(g * 512, n)

def pack4(w):
    words, scales = pack_weight(w, "e2m1")
    return words.reshape(words.shape[0], 128, -1), scales


def unpack4(words, scales):
    return unpack_weight(words.reshape(words.shape[0], 128, -1, 2), scales, "e2m1")


B, NH, T, D, N, CK = 1, 4, 512, 512, 128, 512
KD = NH * N
EPS_LN = 1e-5
TARGET_ACTIVITY = 0.1


def layernorm(v):
    m = np.mean(v, axis=-1, keepdims=True)
    var = np.mean((v - m) ** 2, axis=-1, keepdims=True)
    return (v - m) / np.sqrt(var + EPS_LN)


def setup_inputs():
    t = mx_kscale(KD)
    xy = np.maximum(np.random.standard_normal((B, NH, T, N)) * 0.5, 0.0) * np.maximum(np.random.standard_normal((B, NH, T, N)), 0.0)
    xy_sparse = bf(xy * t.reshape(NH, 1, N))
    decoder_words, decoder_scales = pack4(np.random.standard_normal((KD, D)) * 2.0 / np.sqrt(KD) / t[:, None])
    return {'xy_sparse': xy_sparse,
            'decoder_words': decoder_words,
            'decoder_scales': decoder_scales,
            'x': bf(np.random.standard_normal((B, 1, T, D))),
            'scale': bf(1.0 + 0.1 * np.random.standard_normal(D)),
            'running_activity': bf(TARGET_ACTIVITY * np.exp(0.5 * np.random.standard_normal(D)))}


def reference(xy_sparse, decoder_words, decoder_scales, x, scale, running_activity):
    flat = f64(xy_sparse).transpose(0, 2, 1, 3).reshape(B, 1, T, KD)
    y_mlp = mxq(flat, 3, 'e4m3') @ unpack4(decoder_words, decoder_scales)
    y = layernorm(y_mlp)
    regulation = TARGET_ACTIVITY / (f64(running_activity) + 1e-6)
    y = y * np.sqrt(regulation) * f64(scale)
    return layernorm(f64(x) + y)

@@ -1,0 +1,210 @@
+import concourse.mybir as mybir
+from concourse.masks import make_identity
+
+F32 = mybir.dt.float32
+BF16 = mybir.dt.bfloat16
+I32 = mybir.dt.int32
+U8 = mybir.dt.uint8
+U32 = mybir.dt.uint32
+FP8X4 = mybir.dt.float8_e4m3fn_x4
+FP4X4 = mybir.dt.float4_e2m1fn_x4
+ACT = mybir.ActivationFunctionType
+ALU = mybir.AluOpType
+
+P = 128
+HEADS = 4
+HEAD_DIM = 128
+K = HEADS * HEAD_DIM
+TOKENS = 512
+D = 512
+TILES = TOKENS // P
+WORD_HALVES = 2
+QUADRANTS = 4
+EPS_LN = 1e-5
+TARGET_ACTIVITY = 0.1
+EPS_ACTIVITY = 1e-6
+
+FLOPS = 2 * TOKENS * K * D
+
+
+def tile_bdhlayer_pc_s_kernel(
+    tc, xy_sparse, decoder_words, decoder_scales, x, scale, running_activity, out
+):
+    nc = tc.nc
+
+    xy_tiles = xy_sparse[0].rearrange("h (p i) n -> i p h n", i=TILES)
+    x_rows = x[0, 0].rearrange("(p i) d -> p (i d)", i=TILES)
+    out_tiles = out[0, 0].rearrange("(p i) d -> i p d", i=TILES)
+
+    with tc.tile_pool(name="const", bufs=1) as const, tc.tile_pool(
+        name="per_tile", bufs=TILES
+    ) as per_tile, tc.psum_pool(name="psum_y", bufs=TILES) as psum_y, tc.psum_pool(
+        name="psum_xt", bufs=2
+    ) as psum_xt, tc.psum_pool(name="psum_gain", bufs=1) as psum_gain:
+        w_scales = const.tile([P, D], U8, align_bytes=64)
+        nc.vector.memset(w_scales[:].bitcast(I32), 0)
+        vec_rows = const.tile([P, P], BF16)
+        nc.vector.memset(vec_rows[:], 0.0)
+        one = const.tile([P, 1], F32)
+        nc.vector.memset(one[:], 1.0)
+        table_warm = const.tile([P, 1], F32)
+        nc.scalar.activation(out=table_warm[:], in_=one[:], func=ACT.Abs_reciprocal_sqrt)
+
+        ident_f32 = const.tile([P, P], F32)
+        make_identity(nc, ident_f32[:])
+        ident_bf16 = const.tile([P, P], BF16)
+        make_identity(nc, ident_bf16[:])
+
+        vec_chunks = D // P
+        nc.scalar.dma_start(
+            out=vec_rows[0:vec_chunks, :],
+            in_=running_activity.rearrange("(r c) -> r c", c=P),
+        )
+        nc.scalar.dma_start(
+            out=vec_rows[vec_chunks : 2 * vec_chunks, :],
+            in_=scale.rearrange("(r c) -> r c", c=P),
+        )
+
+        xy_sb = []
+        for i in range(TILES):
+            xy_sb.append(per_tile.tile([P, HEADS, HEAD_DIM], BF16, name="xy_sb"))
+        w_words = const.tile([P, 2 * D], U8, align_bytes=64)
+        x_sb = const.tile([P, TILES, D], BF16)
+
+        nc.sync.dma_start(out=xy_sb[0][:], in_=xy_tiles[0])
+        for q in range(QUADRANTS):
+            nc.sync.dma_start(
+                out=w_scales[32 * q : 32 * q + 4, :].bitcast(I32),
+                in_=decoder_scales[0, 4 * q : 4 * q + 4, :].bitcast(I32),
+            )
+        nc.sync.dma_start(out=w_words[:].bitcast(I32), in_=decoder_words[0].bitcast(I32))
+        nc.sync.dma_start(out=xy_sb[1][:], in_=xy_tiles[1])
+        nc.sync.dma_start(out=x_sb[:].rearrange("p i d -> p (i d)"), in_=x_rows)
+        nc.sync.dma_start(out=xy_sb[2][:], in_=xy_tiles[2])
+        nc.sync.dma_start(out=xy_sb[3][:], in_=xy_tiles[3])
+
+        vec_cols = psum_gain.tile([P, P], BF16)
+        nc.tensor.transpose(vec_cols[:], vec_rows[:], ident_bf16[:])
+        regulation = const.tile([P, vec_chunks], F32)
+        nc.scalar.activation(
+            out=regulation[:],
+            in_=vec_cols[:, 0:vec_chunks],
+            func=ACT.Abs_reciprocal_sqrt,
+            scale=1.0 / TARGET_ACTIVITY,
+            bias=EPS_ACTIVITY / TARGET_ACTIVITY,
+        )
+        gain_cols = const.tile([P, vec_chunks], F32)
+        nc.vector.tensor_tensor(
+            out=gain_cols[:],
+            in0=regulation[:],
+            in1=vec_cols[:, vec_chunks : 2 * vec_chunks],
+            op=ALU.mult,
+        )
+        gain_ps = psum_gain.tile([P, D], F32)
+        for r in range(vec_chunks):
+            nc.tensor.transpose(
+                gain_ps[:, r * P : (r + 1) * P],
+                gain_cols[:, r : r + 1].to_broadcast([P, P]),
+                ident_f32[:],
+            )
+        gain = const.tile([P, D], F32)
+
+        y_ps = []
+
+        def transpose_tile(i):
+            words = xy_sb[i][:].rearrange("p h n -> p (h n)").bitcast(F32)
+            xt = psum_xt.tile([P, WORD_HALVES, P], F32, name="xt")
+            for u in range(WORD_HALVES):
+                nc.tensor.transpose(xt[:, u, :], words[:, u : K // 2 : WORD_HALVES], ident_f32[:])
+            grouped = per_tile.tile([P, P, WORD_HALVES], F32, name="grouped", align_bytes=64)
+            nc.scalar.copy(out=grouped[:], in_=xt[:].rearrange("p u m -> p m u"))
+            return grouped
+
+        def multiply_tile(grouped):
+            codes = per_tile.tile([P, P], U32, name="codes", align_bytes=64)
+            code_scales = per_tile.tile([P, P], U8, name="code_scales", align_bytes=64)
+            nc.vector.quantize_mx(
+                out=codes[:].bitcast(FP8X4),
+                scales=code_scales[:],
+                in_=grouped[:].rearrange("p m u -> p (m u)").bitcast(BF16),
+            )
+            y = psum_y.tile([P, D], F32, name="y")
+            nc.tensor.matmul_mx(
+                out=y[:],
+                lhsT=codes[:].bitcast(FP8X4),
+                lhsT_scale=code_scales[:],
+                rhs=w_words[:].bitcast(FP4X4),
+                rhs_scale=w_scales[:],
+                start=True,
+                stop=True,
+            )
+            return y
+
+        def first_norm_stats(y):
+            stats = per_tile.tile([P, 6], F32, name="stats")
+            nc.vector.bn_stats(out=stats[:], in_=y[:])
+            mean_var = per_tile.tile([P, 2], F32, name="mean_var")
+            nc.vector.bn_aggr(out=mean_var[:], in_=stats[:])
+            rstd = per_tile.tile([P, 1], F32, name="rstd")
+            nc.scalar.activation(
+                out=rstd[:], in_=mean_var[:, 1:2], func=ACT.Abs_reciprocal_sqrt, bias=EPS_LN
+            )
+            return mean_var, rstd
+
+        def second_norm_and_store(i, z, z_sum):
+            neg_mean = per_tile.tile([P, 1], F32, name="neg_mean")
+            nc.scalar.mul(out=neg_mean[:], in_=z_sum[:], mul=-1.0 / D)
+            squares = per_tile.tile([P, D], F32, name="squares")
+            sum_squares = per_tile.tile([P, 1], F32, name="sum_squares")
+            nc.scalar.activation(
+                out=squares[:],
+                in_=z[:],
+                func=ACT.Square,
+                bias=neg_mean[:],
+                accum_out=sum_squares[:],
+            )
+            rstd2 = per_tile.tile([P, 1], F32, name="rstd2")
+            nc.scalar.activation(
+                out=rstd2[:],
+                in_=sum_squares[:],
+                func=ACT.Abs_reciprocal_sqrt,
+                scale=1.0 / D,
+                bias=EPS_LN,
+            )
+            shift = per_tile.tile([P, 1], F32, name="shift")
+            nc.scalar.activation(out=shift[:], in_=neg_mean[:], func=ACT.Copy, scale=rstd2[:])
+            result = per_tile.tile([P, D], F32, name="result")
+            nc.scalar.activation(
+                out=result[:], in_=z[:], func=ACT.Identity, scale=rstd2[:], bias=shift[:]
+            )
+            nc.sync.dma_start(out=out_tiles[i], in_=result[:])
+
+        y_ps.append(multiply_tile(transpose_tile(0)))
+        nc.vector.tensor_copy(out=gain[:], in_=gain_ps[:])
+        for i in range(TILES):
+            if i + 1 < TILES:
+                grouped_next = transpose_tile(i + 1)
+            mean_var, rstd = first_norm_stats(y_ps[i])
+            centred = per_tile.tile([P, D], F32, name="centred")
+            nc.vector.scalar_tensor_tensor(
+                out=centred[:],
+                in0=y_ps[i][:],
+                scalar=mean_var[:, 0:1],
+                in1=gain[:],
+                op0=ALU.subtract,
+                op1=ALU.mult,
+            )
+            if i + 1 < TILES:
+                y_ps.append(multiply_tile(grouped_next))
+            z = per_tile.tile([P, D], F32, name="z")
+            z_sum = per_tile.tile([P, 1], F32, name="z_sum")
+            nc.vector.scalar_tensor_tensor(
+                out=z[:],
+                in0=centred[:],
+                scalar=rstd[:],
+                in1=x_sb[:, i, :],
+                op0=ALU.mult,
+                op1=ALU.add,
+                accum_out=z_sum[:],
+            )
+            second_norm_and_store(i, z, z_sum)

@@ -40,22 +40,11 @@ def tile_bdhlayer_pc_s_kernel(
         name="per_tile", bufs=TILES
     ) as per_tile, tc.psum_pool(name="psum_y", bufs=TILES) as psum_y, tc.psum_pool(
         name="psum_xt", bufs=2
-    ) as psum_xt, tc.psum_pool(name="psum_gain", bufs=1) as psum_gain:
-        w_scales = const.tile([P, D], U8, align_bytes=64)
-        nc.vector.memset(w_scales[:].bitcast(I32), 0)
-        vec_rows = const.tile([P, P], BF16)
-        nc.vector.memset(vec_rows[:], 0.0)
-        one = const.tile([P, 1], F32)
-        nc.vector.memset(one[:], 1.0)
-        table_warm = const.tile([P, 1], F32)
-        nc.scalar.activation(out=table_warm[:], in_=one[:], func=ACT.Abs_reciprocal_sqrt)
-
-        ident_f32 = const.tile([P, P], F32)
-        make_identity(nc, ident_f32[:])
-        ident_bf16 = const.tile([P, P], BF16)
-        make_identity(nc, ident_bf16[:])
+    ) as psum_xt, tc.psum_pool(name="psum_gain", bufs=1) as psum_gain, tc.manual_schedule():
 
         vec_chunks = D // P
+        vec_rows = const.tile([P, P], BF16)
+        nc.vector.memset(vec_rows[:], 0.0)
         nc.scalar.dma_start(
             out=vec_rows[0:vec_chunks, :],
             in_=running_activity.rearrange("(r c) -> r c", c=P),
@@ -64,6 +53,8 @@ def tile_bdhlayer_pc_s_kernel(
             out=vec_rows[vec_chunks : 2 * vec_chunks, :],
             in_=scale.rearrange("(r c) -> r c", c=P),
         )
+        w_scales = const.tile([P, D], U8, align_bytes=64)
+        nc.vector.memset(w_scales[:].bitcast(I32), 0)
 
         xy_sb = []
         for i in range(TILES):
@@ -79,37 +70,18 @@ def tile_bdhlayer_pc_s_kernel(
             )
         nc.sync.dma_start(out=w_words[:].bitcast(I32), in_=decoder_words[0].bitcast(I32))
         nc.sync.dma_start(out=xy_sb[1][:], in_=xy_tiles[1])
-        nc.sync.dma_start(out=x_sb[:].rearrange("p i d -> p (i d)"), in_=x_rows)
         nc.sync.dma_start(out=xy_sb[2][:], in_=xy_tiles[2])
+        nc.sync.dma_start(out=x_sb[:].rearrange("p i d -> p (i d)"), in_=x_rows)
         nc.sync.dma_start(out=xy_sb[3][:], in_=xy_tiles[3])
 
-        vec_cols = psum_gain.tile([P, P], BF16)
-        nc.tensor.transpose(vec_cols[:], vec_rows[:], ident_bf16[:])
-        regulation = const.tile([P, vec_chunks], F32)
-        nc.scalar.activation(
-            out=regulation[:],
-            in_=vec_cols[:, 0:vec_chunks],
-            func=ACT.Abs_reciprocal_sqrt,
-            scale=1.0 / TARGET_ACTIVITY,
-            bias=EPS_ACTIVITY / TARGET_ACTIVITY,
-        )
-        gain_cols = const.tile([P, vec_chunks], F32)
-        nc.vector.tensor_tensor(
-            out=gain_cols[:],
-            in0=regulation[:],
-            in1=vec_cols[:, vec_chunks : 2 * vec_chunks],
-            op=ALU.mult,
-        )
-        gain_ps = psum_gain.tile([P, D], F32)
-        for r in range(vec_chunks):
-            nc.tensor.transpose(
-                gain_ps[:, r * P : (r + 1) * P],
-                gain_cols[:, r : r + 1].to_broadcast([P, P]),
-                ident_f32[:],
-            )
-        gain = const.tile([P, D], F32)
-
-        y_ps = []
+        ident_f32 = const.tile([P, P], F32)
+        make_identity(nc, ident_f32[:])
+        ident_bf16 = const.tile([P, P], BF16)
+        make_identity(nc, ident_bf16[:])
+        one = const.tile([P, 1], F32)
+        nc.vector.memset(one[:], 1.0)
+        table_warm = const.tile([P, 1], F32)
+        nc.scalar.activation(out=table_warm[:], in_=one[:], func=ACT.Abs_reciprocal_sqrt)
 
         def transpose_tile(i):
             words = xy_sb[i][:].rearrange("p h n -> p (h n)").bitcast(F32)
@@ -117,7 +89,8 @@ def tile_bdhlayer_pc_s_kernel(
             for u in range(WORD_HALVES):
                 nc.tensor.transpose(xt[:, u, :], words[:, u : K // 2 : WORD_HALVES], ident_f32[:])
             grouped = per_tile.tile([P, P, WORD_HALVES], F32, name="grouped", align_bytes=64)
-            nc.scalar.copy(out=grouped[:], in_=xt[:].rearrange("p u m -> p m u"))
+            copy_out = nc.vector.tensor_copy if i == 0 else nc.scalar.copy
+            copy_out(out=grouped[:], in_=xt[:].rearrange("p u m -> p m u"))
             return grouped
 
         def multiply_tile(grouped):
@@ -140,62 +113,37 @@ def tile_bdhlayer_pc_s_kernel(
             )
             return y
 
-        def first_norm_stats(y):
-            stats = per_tile.tile([P, 6], F32, name="stats")
-            nc.vector.bn_stats(out=stats[:], in_=y[:])
-            mean_var = per_tile.tile([P, 2], F32, name="mean_var")
-            nc.vector.bn_aggr(out=mean_var[:], in_=stats[:])
-            rstd = per_tile.tile([P, 1], F32, name="rstd")
-            nc.scalar.activation(
-                out=rstd[:], in_=mean_var[:, 1:2], func=ACT.Abs_reciprocal_sqrt, bias=EPS_LN
-            )
-            return mean_var, rstd
-
-        def second_norm_and_store(i, z, z_sum):
-            neg_mean = per_tile.tile([P, 1], F32, name="neg_mean")
-            nc.scalar.mul(out=neg_mean[:], in_=z_sum[:], mul=-1.0 / D)
+        def scalar_mean_rstd(values, total):
+            mean = per_tile.tile([P, 1], F32, name="mean")
+            nc.scalar.mul(out=mean[:], in_=total[:], mul=1.0 / D)
             squares = per_tile.tile([P, D], F32, name="squares")
             sum_squares = per_tile.tile([P, 1], F32, name="sum_squares")
             nc.scalar.activation(
                 out=squares[:],
-                in_=z[:],
+                in_=values[:],
                 func=ACT.Square,
-                bias=neg_mean[:],
+                scale=-1.0,
+                bias=mean[:],
                 accum_out=sum_squares[:],
             )
-            rstd2 = per_tile.tile([P, 1], F32, name="rstd2")
+            rstd = per_tile.tile([P, 1], F32, name="rstd")
             nc.scalar.activation(
-                out=rstd2[:],
+                out=rstd[:],
                 in_=sum_squares[:],
                 func=ACT.Abs_reciprocal_sqrt,
                 scale=1.0 / D,
                 bias=EPS_LN,
             )
-            shift = per_tile.tile([P, 1], F32, name="shift")
-            nc.scalar.activation(out=shift[:], in_=neg_mean[:], func=ACT.Copy, scale=rstd2[:])
-            result = per_tile.tile([P, D], F32, name="result")
-            nc.scalar.activation(
-                out=result[:], in_=z[:], func=ACT.Identity, scale=rstd2[:], bias=shift[:]
-            )
-            nc.sync.dma_start(out=out_tiles[i], in_=result[:])
+            return mean, rstd
 
-        y_ps.append(multiply_tile(transpose_tile(0)))
-        nc.vector.tensor_copy(out=gain[:], in_=gain_ps[:])
-        for i in range(TILES):
-            if i + 1 < TILES:
-                grouped_next = transpose_tile(i + 1)
-            mean_var, rstd = first_norm_stats(y_ps[i])
+        def centre_and_gain(y, mean):
             centred = per_tile.tile([P, D], F32, name="centred")
             nc.vector.scalar_tensor_tensor(
-                out=centred[:],
-                in0=y_ps[i][:],
-                scalar=mean_var[:, 0:1],
-                in1=gain[:],
-                op0=ALU.subtract,
-                op1=ALU.mult,
+                out=centred[:], in0=y[:], scalar=mean, in1=gain[:], op0=ALU.subtract, op1=ALU.mult
             )
-            if i + 1 < TILES:
-                y_ps.append(multiply_tile(grouped_next))
+            return centred
+
+        def add_residual(i, centred, rstd):
             z = per_tile.tile([P, D], F32, name="z")
             z_sum = per_tile.tile([P, 1], F32, name="z_sum")
             nc.vector.scalar_tensor_tensor(
@@ -207,4 +155,74 @@ def tile_bdhlayer_pc_s_kernel(
                 op1=ALU.add,
                 accum_out=z_sum[:],
             )
-            second_norm_and_store(i, z, z_sum)
+            mean2, rstd2 = scalar_mean_rstd(z, z_sum)
+            return z, mean2, rstd2
+
+        def normalise_and_store(i, z, mean2, rstd2):
+            result = per_tile.tile([P, D], F32, name="result")
+            nc.vector.tensor_scalar(
+                out=result[:],
+                in0=z[:],
+                scalar1=mean2[:],
+                scalar2=rstd2[:],
+                op0=ALU.subtract,
+                op1=ALU.mult,
+            )
+            nc.sync.dma_start(out=out_tiles[i], in_=result[:])
+
+        vec_cols = psum_gain.tile([P, P], BF16)
+        nc.tensor.transpose(vec_cols[:], vec_rows[:], ident_bf16[:])
+        regulation = const.tile([P, vec_chunks], F32)
+        nc.scalar.activation(
+            out=regulation[:],
+            in_=vec_cols[:, 0:vec_chunks],
+            func=ACT.Abs_reciprocal_sqrt,
+            scale=1.0 / TARGET_ACTIVITY,
+            bias=EPS_ACTIVITY / TARGET_ACTIVITY,
+        )
+        gain_cols = const.tile([P, vec_chunks], F32)
+        nc.vector.tensor_tensor(
+            out=gain_cols[:],
+            in0=regulation[:],
+            in1=vec_cols[:, vec_chunks : 2 * vec_chunks],
+            op=ALU.mult,
+        )
+
+        grouped = {0: transpose_tile(0)}
+
+        gain_ps = psum_gain.tile([P, D], F32)
+        for r in range(vec_chunks):
+            nc.tensor.transpose(
+                gain_ps[:, r * P : (r + 1) * P],
+                gain_cols[:, r : r + 1].to_broadcast([P, P]),
+                ident_f32[:],
+            )
+        gain = const.tile([P, D], F32)
+        nc.scalar.copy(out=gain[:], in_=gain_ps[:])
+
+        y_ps = {0: multiply_tile(grouped[0])}
+        grouped[1] = transpose_tile(1)
+
+        centred = {}
+        rstd = {}
+        normed = {}
+        for i in range(TILES):
+            if i + 2 < TILES:
+                grouped[i + 2] = transpose_tile(i + 2)
+            stats = per_tile.tile([P, 6], F32, name="stats")
+            nc.vector.bn_stats(out=stats[:], in_=y_ps[i][:])
+            if i + 1 < TILES:
+                y_ps[i + 1] = multiply_tile(grouped[i + 1])
+            mean_var = per_tile.tile([P, 2], F32, name="mean_var")
+            nc.vector.bn_aggr(out=mean_var[:], in_=stats[:])
+            rstd[i] = per_tile.tile([P, 1], F32, name="rstd1")
+            nc.scalar.activation(
+                out=rstd[i][:], in_=mean_var[:, 1:2], func=ACT.Abs_reciprocal_sqrt, bias=EPS_LN
+            )
+            if i >= 1:
+                normed[i - 1] = add_residual(i - 1, centred[i - 1], rstd[i - 1])
+            centred[i] = centre_and_gain(y_ps[i], mean_var[:, 0:1])
+        normed[TILES - 1] = add_residual(TILES - 1, centred[TILES - 1], rstd[TILES - 1])
+
+        for i in range(TILES):
+            normalise_and_store(i, *normed[i])

@@ -114,24 +114,24 @@ def tile_bdhlayer_pc_s_kernel(
             return y
 
         def scalar_mean_rstd(values, total):
-            mean = per_tile.tile([P, 1], F32, name="mean")
-            nc.scalar.mul(out=mean[:], in_=total[:], mul=1.0 / D)
             squares = per_tile.tile([P, D], F32, name="squares")
             sum_squares = per_tile.tile([P, 1], F32, name="sum_squares")
             nc.scalar.activation(
                 out=squares[:],
                 in_=values[:],
                 func=ACT.Square,
-                scale=-1.0,
-                bias=mean[:],
+                scale=-1.0 * D,
+                bias=total[:],
                 accum_out=sum_squares[:],
             )
+            mean = per_tile.tile([P, 1], F32, name="mean")
+            nc.scalar.mul(out=mean[:], in_=total[:], mul=1.0 / D)
             rstd = per_tile.tile([P, 1], F32, name="rstd")
             nc.scalar.activation(
                 out=rstd[:],
                 in_=sum_squares[:],
                 func=ACT.Abs_reciprocal_sqrt,
-                scale=1.0 / D,
+                scale=1.0 / (D * D * D),
                 bias=EPS_LN,
             )
             return mean, rstd
@@ -158,9 +158,9 @@ def tile_bdhlayer_pc_s_kernel(
             mean2, rstd2 = scalar_mean_rstd(z, z_sum)
             return z, mean2, rstd2
 
-        def normalise_and_store(i, z, mean2, rstd2):
+        def normalise_and_store(engine, i, z, mean2, rstd2):
             result = per_tile.tile([P, D], F32, name="result")
-            nc.vector.tensor_scalar(
+            engine.tensor_scalar(
                 out=result[:],
                 in0=z[:],
                 scalar1=mean2[:],
@@ -222,7 +222,9 @@ def tile_bdhlayer_pc_s_kernel(
             if i >= 1:
                 normed[i - 1] = add_residual(i - 1, centred[i - 1], rstd[i - 1])
             centred[i] = centre_and_gain(y_ps[i], mean_var[:, 0:1])
+            if i >= 2:
+                normalise_and_store(nc.gpsimd, i - 2, *normed[i - 2])
         normed[TILES - 1] = add_residual(TILES - 1, centred[TILES - 1], rstd[TILES - 1])
 
-        for i in range(TILES):
-            normalise_and_store(i, *normed[i])
+        for i in range(TILES - 2, TILES):
+            normalise_and_store(nc.vector, i, *normed[i])

@@ -20,6 +20,7 @@ D = 512
 TILES = TOKENS // P
 WORD_HALVES = 2
 QUADRANTS = 4
+SCALAR_OUTPUT_TILES = 1
 EPS_LN = 1e-5
 TARGET_ACTIVITY = 0.1
 EPS_ACTIVITY = 1e-6
@@ -124,8 +125,8 @@ def tile_bdhlayer_pc_s_kernel(
                 bias=total[:],
                 accum_out=sum_squares[:],
             )
-            mean = per_tile.tile([P, 1], F32, name="mean")
-            nc.scalar.mul(out=mean[:], in_=total[:], mul=1.0 / D)
+            neg_mean = per_tile.tile([P, 1], F32, name="neg_mean")
+            nc.scalar.mul(out=neg_mean[:], in_=total[:], mul=-1.0 / D)
             rstd = per_tile.tile([P, 1], F32, name="rstd")
             nc.scalar.activation(
                 out=rstd[:],
@@ -134,7 +135,7 @@ def tile_bdhlayer_pc_s_kernel(
                 scale=1.0 / (D * D * D),
                 bias=EPS_LN,
             )
-            return mean, rstd
+            return neg_mean, rstd
 
         def centre_and_gain(y, mean):
             centred = per_tile.tile([P, D], F32, name="centred")
@@ -155,18 +156,27 @@ def tile_bdhlayer_pc_s_kernel(
                 op1=ALU.add,
                 accum_out=z_sum[:],
             )
-            mean2, rstd2 = scalar_mean_rstd(z, z_sum)
-            return z, mean2, rstd2
+            neg_mean2, rstd2 = scalar_mean_rstd(z, z_sum)
+            return z, neg_mean2, rstd2
 
-        def normalise_and_store(engine, i, z, mean2, rstd2):
+        def vector_normalise_and_store(i, z, neg_mean2, rstd2):
             result = per_tile.tile([P, D], F32, name="result")
-            engine.tensor_scalar(
+            nc.vector.tensor_scalar(
                 out=result[:],
                 in0=z[:],
-                scalar1=mean2[:],
+                scalar1=neg_mean2[:],
                 scalar2=rstd2[:],
-                op0=ALU.subtract,
+                op0=ALU.add,
                 op1=ALU.mult,
+            )
+            nc.sync.dma_start(out=out_tiles[i], in_=result[:])
+
+        def scalar_normalise_and_store(i, z, neg_mean2, rstd2):
+            shift = per_tile.tile([P, 1], F32, name="shift")
+            nc.scalar.activation(out=shift[:], in_=neg_mean2[:], func=ACT.Copy, scale=rstd2[:])
+            result = per_tile.tile([P, D], F32, name="result")
+            nc.scalar.activation(
+                out=result[:], in_=z[:], func=ACT.Identity, scale=rstd2[:], bias=shift[:]
             )
             nc.sync.dma_start(out=out_tiles[i], in_=result[:])
 
@@ -219,12 +229,12 @@ def tile_bdhlayer_pc_s_kernel(
             nc.scalar.activation(
                 out=rstd[i][:], in_=mean_var[:, 1:2], func=ACT.Abs_reciprocal_sqrt, bias=EPS_LN
             )
+            if 0 <= i - 2 < SCALAR_OUTPUT_TILES:
+                scalar_normalise_and_store(i - 2, *normed[i - 2])
             if i >= 1:
                 normed[i - 1] = add_residual(i - 1, centred[i - 1], rstd[i - 1])
             centred[i] = centre_and_gain(y_ps[i], mean_var[:, 0:1])
-            if i >= 2:
-                normalise_and_store(nc.gpsimd, i - 2, *normed[i - 2])
         normed[TILES - 1] = add_residual(TILES - 1, centred[TILES - 1], rstd[TILES - 1])
 
-        for i in range(TILES - 2, TILES):
-            normalise_and_store(nc.vector, i, *normed[i])
+        for i in range(SCALAR_OUTPUT_TILES, TILES):
+            vector_normalise_and_store(i, *normed[i])

@@ -21,6 +21,7 @@ TILES = TOKENS // P
 WORD_HALVES = 2
 QUADRANTS = 4
 SCALAR_OUTPUT_TILES = 1
+SCALAR_STATS_TILES = (3,)
 EPS_LN = 1e-5
 TARGET_ACTIVITY = 0.1
 EPS_ACTIVITY = 1e-6
@@ -72,8 +73,8 @@ def tile_bdhlayer_pc_s_kernel(
         nc.sync.dma_start(out=w_words[:].bitcast(I32), in_=decoder_words[0].bitcast(I32))
         nc.sync.dma_start(out=xy_sb[1][:], in_=xy_tiles[1])
         nc.sync.dma_start(out=xy_sb[2][:], in_=xy_tiles[2])
-        nc.sync.dma_start(out=x_sb[:].rearrange("p i d -> p (i d)"), in_=x_rows)
         nc.sync.dma_start(out=xy_sb[3][:], in_=xy_tiles[3])
+        nc.sync.dma_start(out=x_sb[:].rearrange("p i d -> p (i d)"), in_=x_rows)
 
         ident_f32 = const.tile([P, P], F32)
         make_identity(nc, ident_f32[:])
@@ -137,12 +138,18 @@ def tile_bdhlayer_pc_s_kernel(
             )
             return neg_mean, rstd
 
-        def centre_and_gain(y, mean):
+        def centre_and_gain(y, mean, op0=ALU.subtract):
             centred = per_tile.tile([P, D], F32, name="centred")
             nc.vector.scalar_tensor_tensor(
-                out=centred[:], in0=y[:], scalar=mean, in1=gain[:], op0=ALU.subtract, op1=ALU.mult
+                out=centred[:], in0=y[:], scalar=mean, in1=gain[:], op0=op0, op1=ALU.mult
             )
             return centred
+
+        def scalar_first_norm(y):
+            copied = per_tile.tile([P, D], F32, name="squares")
+            total = per_tile.tile([P, 1], F32, name="y_sum")
+            nc.scalar.activation(out=copied[:], in_=y[:], func=ACT.Identity, accum_out=total[:])
+            return scalar_mean_rstd(y, total)
 
         def add_residual(i, centred, rstd):
             z = per_tile.tile([P, D], F32, name="z")
@@ -216,25 +223,47 @@ def tile_bdhlayer_pc_s_kernel(
         centred = {}
         rstd = {}
         normed = {}
-        for i in range(TILES):
-            if i + 2 < TILES:
-                grouped[i + 2] = transpose_tile(i + 2)
-            stats = per_tile.tile([P, 6], F32, name="stats")
-            nc.vector.bn_stats(out=stats[:], in_=y_ps[i][:])
-            if i + 1 < TILES:
-                y_ps[i + 1] = multiply_tile(grouped[i + 1])
+        stats = {}
+        mean = {}
+
+        def vector_stats(i):
+            stats[i] = per_tile.tile([P, 6], F32, name="stats")
+            nc.vector.bn_stats(out=stats[i][:], in_=y_ps[i][:])
+
+        def vector_aggregate(i):
             mean_var = per_tile.tile([P, 2], F32, name="mean_var")
-            nc.vector.bn_aggr(out=mean_var[:], in_=stats[:])
+            nc.vector.bn_aggr(out=mean_var[:], in_=stats[i][:])
+            mean[i] = mean_var[:, 0:1]
             rstd[i] = per_tile.tile([P, 1], F32, name="rstd1")
             nc.scalar.activation(
                 out=rstd[i][:], in_=mean_var[:, 1:2], func=ACT.Abs_reciprocal_sqrt, bias=EPS_LN
             )
-            if 0 <= i - 2 < SCALAR_OUTPUT_TILES:
-                scalar_normalise_and_store(i - 2, *normed[i - 2])
-            if i >= 1:
-                normed[i - 1] = add_residual(i - 1, centred[i - 1], rstd[i - 1])
-            centred[i] = centre_and_gain(y_ps[i], mean_var[:, 0:1])
-        normed[TILES - 1] = add_residual(TILES - 1, centred[TILES - 1], rstd[TILES - 1])
 
-        for i in range(SCALAR_OUTPUT_TILES, TILES):
+        grouped[2] = transpose_tile(2)
+        vector_stats(0)
+        y_ps[1] = multiply_tile(grouped[1])
+        vector_aggregate(0)
+        centred[0] = centre_and_gain(y_ps[0], mean[0])
+
+        grouped[3] = transpose_tile(3)
+        vector_stats(1)
+        y_ps[2] = multiply_tile(grouped[2])
+        vector_aggregate(1)
+        y_ps[3] = multiply_tile(grouped[3])
+        copied = per_tile.tile([P, D], F32, name="squares")
+        y3_sum = per_tile.tile([P, 1], F32, name="y_sum")
+        nc.scalar.activation(out=copied[:], in_=y_ps[3][:], func=ACT.Identity, accum_out=y3_sum[:])
+        normed[0] = add_residual(0, centred[0], rstd[0])
+        neg_mean3, rstd[3] = scalar_mean_rstd(y_ps[3], y3_sum)
+        centred[1] = centre_and_gain(y_ps[1], mean[1])
+
+        vector_stats(2)
+        normed[1] = add_residual(1, centred[1], rstd[1])
+        vector_aggregate(2)
+        scalar_normalise_and_store(0, *normed[0])
+        centred[3] = centre_and_gain(y_ps[3], neg_mean3[:], op0=ALU.add)
+        centred[2] = centre_and_gain(y_ps[2], mean[2])
+        normed[3] = add_residual(3, centred[3], rstd[3])
+        normed[2] = add_residual(2, centred[2], rstd[2])
+        for i in (1, 3, 2):
             vector_normalise_and_store(i, *normed[i])

@@ -73,8 +73,8 @@ def tile_bdhlayer_pc_s_kernel(
         nc.sync.dma_start(out=w_words[:].bitcast(I32), in_=decoder_words[0].bitcast(I32))
         nc.sync.dma_start(out=xy_sb[1][:], in_=xy_tiles[1])
         nc.sync.dma_start(out=xy_sb[2][:], in_=xy_tiles[2])
-        nc.sync.dma_start(out=xy_sb[3][:], in_=xy_tiles[3])
         nc.sync.dma_start(out=x_sb[:].rearrange("p i d -> p (i d)"), in_=x_rows)
+        nc.sync.dma_start(out=xy_sb[3][:], in_=xy_tiles[3])
 
         ident_f32 = const.tile([P, P], F32)
         make_identity(nc, ident_f32[:])
@@ -114,6 +114,20 @@ def tile_bdhlayer_pc_s_kernel(
                 stop=True,
             )
             return y
+
+        def vector_residual(i, centred_i, rstd_i):
+            z = per_tile.tile([P, D], F32, name="z")
+            z_sum = per_tile.tile([P, 1], F32, name="z_sum")
+            nc.vector.scalar_tensor_tensor(
+                out=z[:],
+                in0=centred_i[:],
+                scalar=rstd_i[:],
+                in1=x_sb[:, i, :],
+                op0=ALU.mult,
+                op1=ALU.add,
+                accum_out=z_sum[:],
+            )
+            return z, z_sum
 
         def scalar_mean_rstd(values, total):
             squares = per_tile.tile([P, D], F32, name="squares")
@@ -249,21 +263,19 @@ def tile_bdhlayer_pc_s_kernel(
         vector_stats(1)
         y_ps[2] = multiply_tile(grouped[2])
         vector_aggregate(1)
-        y_ps[3] = multiply_tile(grouped[3])
-        copied = per_tile.tile([P, D], F32, name="squares")
-        y3_sum = per_tile.tile([P, 1], F32, name="y_sum")
-        nc.scalar.activation(out=copied[:], in_=y_ps[3][:], func=ACT.Identity, accum_out=y3_sum[:])
         normed[0] = add_residual(0, centred[0], rstd[0])
-        neg_mean3, rstd[3] = scalar_mean_rstd(y_ps[3], y3_sum)
+        y_ps[3] = multiply_tile(grouped[3])
+        neg_mean3, rstd[3] = scalar_first_norm(y_ps[3])
         centred[1] = centre_and_gain(y_ps[1], mean[1])
 
         vector_stats(2)
-        normed[1] = add_residual(1, centred[1], rstd[1])
+        z1, z1_sum = vector_residual(1, centred[1], rstd[1])
         vector_aggregate(2)
-        scalar_normalise_and_store(0, *normed[0])
-        centred[3] = centre_and_gain(y_ps[3], neg_mean3[:], op0=ALU.add)
+        normed[1] = (z1,) + scalar_mean_rstd(z1, z1_sum)
+        vector_normalise_and_store(0, *normed[0])
         centred[2] = centre_and_gain(y_ps[2], mean[2])
-        normed[3] = add_residual(3, centred[3], rstd[3])
+        centred[3] = centre_and_gain(y_ps[3], neg_mean3[:], op0=ALU.add)
         normed[2] = add_residual(2, centred[2], rstd[2])
-        for i in (1, 3, 2):
+        normed[3] = add_residual(3, centred[3], rstd[3])
+        for i in range(1, TILES):
             vector_normalise_and_store(i, *normed[i])

@@ -255,15 +255,15 @@ def tile_bdhlayer_pc_s_kernel(
 
         grouped[2] = transpose_tile(2)
         vector_stats(0)
-        y_ps[1] = multiply_tile(grouped[1])
         vector_aggregate(0)
+        y_ps[1] = multiply_tile(grouped[1])
         centred[0] = centre_and_gain(y_ps[0], mean[0])
 
         grouped[3] = transpose_tile(3)
-        vector_stats(1)
         y_ps[2] = multiply_tile(grouped[2])
-        vector_aggregate(1)
+        vector_stats(1)
         normed[0] = add_residual(0, centred[0], rstd[0])
+        vector_aggregate(1)
         y_ps[3] = multiply_tile(grouped[3])
         neg_mean3, rstd[3] = scalar_first_norm(y_ps[3])
         centred[1] = centre_and_gain(y_ps[1], mean[1])

@@ -45,16 +45,12 @@ def tile_bdhlayer_pc_s_kernel(
     ) as psum_xt, tc.psum_pool(name="psum_gain", bufs=1) as psum_gain, tc.manual_schedule():
 
         vec_chunks = D // P
-        vec_rows = const.tile([P, P], BF16)
-        nc.vector.memset(vec_rows[:], 0.0)
+        activity_cols = const.tile([P, vec_chunks], BF16)
+        scale_cols = const.tile([P, vec_chunks], BF16)
         nc.scalar.dma_start(
-            out=vec_rows[0:vec_chunks, :],
-            in_=running_activity.rearrange("(r c) -> r c", c=P),
+            out=activity_cols[:], in_=running_activity.rearrange("(p c) -> p c", c=vec_chunks)
         )
-        nc.scalar.dma_start(
-            out=vec_rows[vec_chunks : 2 * vec_chunks, :],
-            in_=scale.rearrange("(r c) -> r c", c=P),
-        )
+        nc.scalar.dma_start(out=scale_cols[:], in_=scale.rearrange("(p c) -> p c", c=vec_chunks))
         w_scales = const.tile([P, D], U8, align_bytes=64)
         nc.vector.memset(w_scales[:].bitcast(I32), 0)
 
@@ -65,12 +61,12 @@ def tile_bdhlayer_pc_s_kernel(
         x_sb = const.tile([P, TILES, D], BF16)
 
         nc.sync.dma_start(out=xy_sb[0][:], in_=xy_tiles[0])
+        nc.sync.dma_start(out=w_words[:].bitcast(I32), in_=decoder_words[0].bitcast(I32))
         for q in range(QUADRANTS):
             nc.sync.dma_start(
                 out=w_scales[32 * q : 32 * q + 4, :].bitcast(I32),
                 in_=decoder_scales[0, 4 * q : 4 * q + 4, :].bitcast(I32),
             )
-        nc.sync.dma_start(out=w_words[:].bitcast(I32), in_=decoder_words[0].bitcast(I32))
         nc.sync.dma_start(out=xy_sb[1][:], in_=xy_tiles[1])
         nc.sync.dma_start(out=xy_sb[2][:], in_=xy_tiles[2])
         nc.sync.dma_start(out=x_sb[:].rearrange("p i d -> p (i d)"), in_=x_rows)
@@ -78,8 +74,6 @@ def tile_bdhlayer_pc_s_kernel(
 
         ident_f32 = const.tile([P, P], F32)
         make_identity(nc, ident_f32[:])
-        ident_bf16 = const.tile([P, P], BF16)
-        make_identity(nc, ident_bf16[:])
         one = const.tile([P, 1], F32)
         nc.vector.memset(one[:], 1.0)
         table_warm = const.tile([P, 1], F32)
@@ -201,12 +195,10 @@ def tile_bdhlayer_pc_s_kernel(
             )
             nc.sync.dma_start(out=out_tiles[i], in_=result[:])
 
-        vec_cols = psum_gain.tile([P, P], BF16)
-        nc.tensor.transpose(vec_cols[:], vec_rows[:], ident_bf16[:])
         regulation = const.tile([P, vec_chunks], F32)
         nc.scalar.activation(
             out=regulation[:],
-            in_=vec_cols[:, 0:vec_chunks],
+            in_=activity_cols[:],
             func=ACT.Abs_reciprocal_sqrt,
             scale=1.0 / TARGET_ACTIVITY,
             bias=EPS_ACTIVITY / TARGET_ACTIVITY,
@@ -215,21 +207,24 @@ def tile_bdhlayer_pc_s_kernel(
         nc.vector.tensor_tensor(
             out=gain_cols[:],
             in0=regulation[:],
-            in1=vec_cols[:, vec_chunks : 2 * vec_chunks],
+            in1=scale_cols[:],
             op=ALU.mult,
         )
 
         grouped = {0: transpose_tile(0)}
 
-        gain_ps = psum_gain.tile([P, D], F32)
-        for r in range(vec_chunks):
+        gain_ps = psum_gain.tile([P, vec_chunks, P], F32)
+        for c in range(vec_chunks):
             nc.tensor.transpose(
-                gain_ps[:, r * P : (r + 1) * P],
-                gain_cols[:, r : r + 1].to_broadcast([P, P]),
+                gain_ps[:, c, :],
+                gain_cols[:, c : c + 1].to_broadcast([P, P]),
                 ident_f32[:],
             )
         gain = const.tile([P, D], F32)
-        nc.scalar.copy(out=gain[:], in_=gain_ps[:])
+        nc.scalar.copy(
+            out=gain[:].rearrange("p (n c) -> p n c", c=vec_chunks),
+            in_=gain_ps[:].rearrange("p c n -> p n c"),
+        )
 
         y_ps = {0: multiply_tile(grouped[0])}
         grouped[1] = transpose_tile(1)
@@ -275,7 +270,24 @@ def tile_bdhlayer_pc_s_kernel(
         vector_normalise_and_store(0, *normed[0])
         centred[2] = centre_and_gain(y_ps[2], mean[2])
         centred[3] = centre_and_gain(y_ps[3], neg_mean3[:], op0=ALU.add)
-        normed[2] = add_residual(2, centred[2], rstd[2])
-        normed[3] = add_residual(3, centred[3], rstd[3])
+        for i in (2, 3):
+            z_i, z_sum_i = vector_residual(i, centred[i], rstd[i])
+            squares = per_tile.tile([P, D], F32, name="squares")
+            sum_squares = per_tile.tile([P, 1], F32, name="sum_squares")
+            nc.scalar.activation(
+                out=squares[:], in_=z_i[:], func=ACT.Square, scale=-1.0 * D, bias=z_sum_i[:],
+                accum_out=sum_squares[:],
+            )
+            rstd2 = per_tile.tile([P, 1], F32, name="rstd")
+            nc.scalar.activation(
+                out=rstd2[:], in_=sum_squares[:], func=ACT.Abs_reciprocal_sqrt,
+                scale=1.0 / (D * D * D), bias=EPS_LN,
+            )
+            normed[i] = (z_i, z_sum_i, rstd2)
+        for i in (2, 3):
+            z_i, z_sum_i, rstd2 = normed[i]
+            neg_mean = per_tile.tile([P, 1], F32, name="neg_mean")
+            nc.vector.tensor_scalar_mul(out=neg_mean[:], in0=z_sum_i[:], scalar1=-1.0 / D)
+            normed[i] = (z_i, neg_mean, rstd2)
         for i in range(1, TILES):
             vector_normalise_and_store(i, *normed[i])

@@ -19,9 +19,8 @@ TOKENS = 512
 D = 512
 TILES = TOKENS // P
 WORD_HALVES = 2
+FOLD = 128
 QUADRANTS = 4
-SCALAR_OUTPUT_TILES = 1
-SCALAR_STATS_TILES = (3,)
 EPS_LN = 1e-5
 TARGET_ACTIVITY = 0.1
 EPS_ACTIVITY = 1e-6
@@ -42,7 +41,9 @@ def tile_bdhlayer_pc_s_kernel(
         name="per_tile", bufs=TILES
     ) as per_tile, tc.psum_pool(name="psum_y", bufs=TILES) as psum_y, tc.psum_pool(
         name="psum_xt", bufs=2
-    ) as psum_xt, tc.psum_pool(name="psum_gain", bufs=1) as psum_gain, tc.manual_schedule():
+    ) as psum_xt, tc.psum_pool(name="psum_gain", bufs=1) as psum_gain, tc.psum_pool(
+        name="psum_fold", bufs=1
+    ) as psum_fold, tc.manual_schedule():
 
         vec_chunks = D // P
         activity_cols = const.tile([P, vec_chunks], BF16)
@@ -79,119 +80,164 @@ def tile_bdhlayer_pc_s_kernel(
         table_warm = const.tile([P, 1], F32)
         nc.scalar.activation(out=table_warm[:], in_=one[:], func=ACT.Abs_reciprocal_sqrt)
 
+        xt, grouped, codes, quarters, y_ps = {}, {}, {}, {}, {}
+        mean, rstd, centred, z, z_sum = {}, {}, {}, {}, {}
+        neg_mean, sum_squares, sum_squares2, neg_mean2, rstd2 = {}, {}, {}, {}, {}
+
+        def column(name):
+            return per_tile.tile([P, 1], F32, name=name)
+
         def transpose_tile(i):
             words = xy_sb[i][:].rearrange("p h n -> p (h n)").bitcast(F32)
-            xt = psum_xt.tile([P, WORD_HALVES, P], F32, name="xt")
+            xt[i] = psum_xt.tile([P, WORD_HALVES, P], F32, name="xt")
             for u in range(WORD_HALVES):
-                nc.tensor.transpose(xt[:, u, :], words[:, u : K // 2 : WORD_HALVES], ident_f32[:])
-            grouped = per_tile.tile([P, P, WORD_HALVES], F32, name="grouped", align_bytes=64)
+                nc.tensor.transpose(
+                    xt[i][:, u, :], words[:, u : K // 2 : WORD_HALVES], ident_f32[:]
+                )
+
+        def copy_tile(i):
+            grouped[i] = per_tile.tile([P, P, WORD_HALVES], F32, name="grouped", align_bytes=64)
             copy_out = nc.vector.tensor_copy if i == 0 else nc.scalar.copy
-            copy_out(out=grouped[:], in_=xt[:].rearrange("p u m -> p m u"))
-            return grouped
+            copy_out(out=grouped[i][:], in_=xt[i][:].rearrange("p u m -> p m u"))
 
-        def multiply_tile(grouped):
-            codes = per_tile.tile([P, P], U32, name="codes", align_bytes=64)
-            code_scales = per_tile.tile([P, P], U8, name="code_scales", align_bytes=64)
+        def quantise(i):
+            codes[i] = (
+                per_tile.tile([P, P], U32, name="codes", align_bytes=64),
+                per_tile.tile([P, P], U8, name="code_scales", align_bytes=64),
+            )
             nc.vector.quantize_mx(
-                out=codes[:].bitcast(FP8X4),
-                scales=code_scales[:],
-                in_=grouped[:].rearrange("p m u -> p (m u)").bitcast(BF16),
+                out=codes[i][0][:].bitcast(FP8X4),
+                scales=codes[i][1][:],
+                in_=grouped[i][:].rearrange("p m u -> p (m u)").bitcast(BF16),
             )
-            y = psum_y.tile([P, D], F32, name="y")
+
+        def decode(i, out, first, last, start, stop):
             nc.tensor.matmul_mx(
-                out=y[:],
-                lhsT=codes[:].bitcast(FP8X4),
-                lhsT_scale=code_scales[:],
-                rhs=w_words[:].bitcast(FP4X4),
-                rhs_scale=w_scales[:],
-                start=True,
-                stop=True,
+                out=out,
+                lhsT=codes[i][0][:].bitcast(FP8X4),
+                lhsT_scale=codes[i][1][:],
+                rhs=w_words[:, 2 * first : 2 * last].bitcast(FP4X4),
+                rhs_scale=w_scales[:, first:last],
+                start=start,
+                stop=stop,
             )
-            return y
 
-        def vector_residual(i, centred_i, rstd_i):
-            z = per_tile.tile([P, D], F32, name="z")
-            z_sum = per_tile.tile([P, 1], F32, name="z_sum")
-            nc.vector.scalar_tensor_tensor(
-                out=z[:],
-                in0=centred_i[:],
-                scalar=rstd_i[:],
-                in1=x_sb[:, i, :],
-                op0=ALU.mult,
-                op1=ALU.add,
-                accum_out=z_sum[:],
+        def multiply(i):
+            y_ps[i] = psum_y.tile([P, D], F32, name="y")
+            decode(i, y_ps[i][:], 0, D, True, True)
+
+        def fold(i):
+            quarters[i] = psum_fold.tile([P, FOLD], F32, name="quarters")
+            for c in range(D // FOLD):
+                decode(
+                    i, quarters[i][:], FOLD * c, FOLD * (c + 1), c == 0, c == D // FOLD - 1
+                )
+
+        def vector_stats(i):
+            stats = per_tile.tile([P, 6], F32, name="stats")
+            nc.vector.bn_stats(out=stats[:], in_=y_ps[i][:])
+            return stats
+
+        def vector_aggregate(i, stats):
+            mean_var = per_tile.tile([P, 2], F32, name="mean_var")
+            nc.vector.bn_aggr(out=mean_var[:], in_=stats[:])
+            mean[i] = mean_var[:, 0:1]
+            rstd[i] = column("rstd1")
+            nc.scalar.activation(
+                out=rstd[i][:], in_=mean_var[:, 1:2], func=ACT.Abs_reciprocal_sqrt, bias=EPS_LN
             )
-            return z, z_sum
 
-        def scalar_mean_rstd(values, total):
+        def scalar_sum(i):
+            copied = per_tile.tile([P, FOLD], F32, name="copied")
+            neg_mean[i] = column("neg_mean")
+            nc.scalar.activation(
+                out=copied[:],
+                in_=quarters[i][:],
+                func=ACT.Identity,
+                scale=-1.0 / D,
+                accum_out=neg_mean[i][:],
+            )
+
+        def scalar_first_squares(i):
             squares = per_tile.tile([P, D], F32, name="squares")
-            sum_squares = per_tile.tile([P, 1], F32, name="sum_squares")
+            sum_squares[i] = column("sum_squares")
             nc.scalar.activation(
                 out=squares[:],
-                in_=values[:],
+                in_=y_ps[i][:],
+                func=ACT.Square,
+                bias=neg_mean[i][:],
+                accum_out=sum_squares[i][:],
+            )
+
+        def scalar_first_rstd(i):
+            rstd[i] = column("rstd1")
+            nc.scalar.activation(
+                out=rstd[i][:],
+                in_=sum_squares[i][:],
+                func=ACT.Abs_reciprocal_sqrt,
+                scale=1.0 / D,
+                bias=EPS_LN,
+            )
+
+        def second_squares(i):
+            squares = per_tile.tile([P, D], F32, name="squares")
+            sum_squares2[i] = column("sum_squares2")
+            nc.scalar.activation(
+                out=squares[:],
+                in_=z[i][:],
                 func=ACT.Square,
                 scale=-1.0 * D,
-                bias=total[:],
-                accum_out=sum_squares[:],
+                bias=z_sum[i][:],
+                accum_out=sum_squares2[i][:],
             )
-            neg_mean = per_tile.tile([P, 1], F32, name="neg_mean")
-            nc.scalar.mul(out=neg_mean[:], in_=total[:], mul=-1.0 / D)
-            rstd = per_tile.tile([P, 1], F32, name="rstd")
+
+        def second_rstd(i):
+            rstd2[i] = column("rstd2")
             nc.scalar.activation(
-                out=rstd[:],
-                in_=sum_squares[:],
+                out=rstd2[i][:],
+                in_=sum_squares2[i][:],
                 func=ACT.Abs_reciprocal_sqrt,
                 scale=1.0 / (D * D * D),
                 bias=EPS_LN,
             )
-            return neg_mean, rstd
 
-        def centre_and_gain(y, mean, op0=ALU.subtract):
-            centred = per_tile.tile([P, D], F32, name="centred")
+        def second_mean(i, engine_mul):
+            neg_mean2[i] = column("neg_mean2")
+            engine_mul(neg_mean2[i][:], z_sum[i][:], -1.0 / D)
+
+        def centre_and_gain(i):
+            centred[i] = per_tile.tile([P, D], F32, name="centred")
             nc.vector.scalar_tensor_tensor(
-                out=centred[:], in0=y[:], scalar=mean, in1=gain[:], op0=op0, op1=ALU.mult
+                out=centred[i][:],
+                in0=y_ps[i][:],
+                scalar=mean[i] if i in mean else neg_mean[i][:],
+                in1=gain[:],
+                op0=ALU.subtract if i in mean else ALU.add,
+                op1=ALU.mult,
             )
-            return centred
 
-        def scalar_first_norm(y):
-            copied = per_tile.tile([P, D], F32, name="squares")
-            total = per_tile.tile([P, 1], F32, name="y_sum")
-            nc.scalar.activation(out=copied[:], in_=y[:], func=ACT.Identity, accum_out=total[:])
-            return scalar_mean_rstd(y, total)
-
-        def add_residual(i, centred, rstd):
-            z = per_tile.tile([P, D], F32, name="z")
-            z_sum = per_tile.tile([P, 1], F32, name="z_sum")
+        def add_residual(i):
+            z[i] = per_tile.tile([P, D], F32, name="z")
+            z_sum[i] = column("z_sum")
             nc.vector.scalar_tensor_tensor(
-                out=z[:],
-                in0=centred[:],
-                scalar=rstd[:],
+                out=z[i][:],
+                in0=centred[i][:],
+                scalar=rstd[i][:],
                 in1=x_sb[:, i, :],
                 op0=ALU.mult,
                 op1=ALU.add,
-                accum_out=z_sum[:],
+                accum_out=z_sum[i][:],
             )
-            neg_mean2, rstd2 = scalar_mean_rstd(z, z_sum)
-            return z, neg_mean2, rstd2
 
-        def vector_normalise_and_store(i, z, neg_mean2, rstd2):
+        def normalise_and_store(i):
             result = per_tile.tile([P, D], F32, name="result")
             nc.vector.tensor_scalar(
                 out=result[:],
-                in0=z[:],
-                scalar1=neg_mean2[:],
-                scalar2=rstd2[:],
+                in0=z[i][:],
+                scalar1=neg_mean2[i][:],
+                scalar2=rstd2[i][:],
                 op0=ALU.add,
                 op1=ALU.mult,
-            )
-            nc.sync.dma_start(out=out_tiles[i], in_=result[:])
-
-        def scalar_normalise_and_store(i, z, neg_mean2, rstd2):
-            shift = per_tile.tile([P, 1], F32, name="shift")
-            nc.scalar.activation(out=shift[:], in_=neg_mean2[:], func=ACT.Copy, scale=rstd2[:])
-            result = per_tile.tile([P, D], F32, name="result")
-            nc.scalar.activation(
-                out=result[:], in_=z[:], func=ACT.Identity, scale=rstd2[:], bias=shift[:]
             )
             nc.sync.dma_start(out=out_tiles[i], in_=result[:])
 
@@ -211,7 +257,8 @@ def tile_bdhlayer_pc_s_kernel(
             op=ALU.mult,
         )
 
-        grouped = {0: transpose_tile(0)}
+        transpose_tile(0)
+        copy_tile(0)
 
         gain_ps = psum_gain.tile([P, vec_chunks, P], F32)
         for c in range(vec_chunks):
@@ -226,68 +273,53 @@ def tile_bdhlayer_pc_s_kernel(
             in_=gain_ps[:].rearrange("p c n -> p n c"),
         )
 
-        y_ps = {0: multiply_tile(grouped[0])}
-        grouped[1] = transpose_tile(1)
-
-        centred = {}
-        rstd = {}
-        normed = {}
-        stats = {}
-        mean = {}
-
-        def vector_stats(i):
-            stats[i] = per_tile.tile([P, 6], F32, name="stats")
-            nc.vector.bn_stats(out=stats[i][:], in_=y_ps[i][:])
-
-        def vector_aggregate(i):
-            mean_var = per_tile.tile([P, 2], F32, name="mean_var")
-            nc.vector.bn_aggr(out=mean_var[:], in_=stats[i][:])
-            mean[i] = mean_var[:, 0:1]
-            rstd[i] = per_tile.tile([P, 1], F32, name="rstd1")
-            nc.scalar.activation(
-                out=rstd[i][:], in_=mean_var[:, 1:2], func=ACT.Abs_reciprocal_sqrt, bias=EPS_LN
-            )
-
-        grouped[2] = transpose_tile(2)
-        vector_stats(0)
-        vector_aggregate(0)
-        y_ps[1] = multiply_tile(grouped[1])
-        centred[0] = centre_and_gain(y_ps[0], mean[0])
-
-        grouped[3] = transpose_tile(3)
-        y_ps[2] = multiply_tile(grouped[2])
-        vector_stats(1)
-        normed[0] = add_residual(0, centred[0], rstd[0])
-        vector_aggregate(1)
-        y_ps[3] = multiply_tile(grouped[3])
-        neg_mean3, rstd[3] = scalar_first_norm(y_ps[3])
-        centred[1] = centre_and_gain(y_ps[1], mean[1])
-
-        vector_stats(2)
-        z1, z1_sum = vector_residual(1, centred[1], rstd[1])
-        vector_aggregate(2)
-        normed[1] = (z1,) + scalar_mean_rstd(z1, z1_sum)
-        vector_normalise_and_store(0, *normed[0])
-        centred[2] = centre_and_gain(y_ps[2], mean[2])
-        centred[3] = centre_and_gain(y_ps[3], neg_mean3[:], op0=ALU.add)
-        for i in (2, 3):
-            z_i, z_sum_i = vector_residual(i, centred[i], rstd[i])
-            squares = per_tile.tile([P, D], F32, name="squares")
-            sum_squares = per_tile.tile([P, 1], F32, name="sum_squares")
-            nc.scalar.activation(
-                out=squares[:], in_=z_i[:], func=ACT.Square, scale=-1.0 * D, bias=z_sum_i[:],
-                accum_out=sum_squares[:],
-            )
-            rstd2 = per_tile.tile([P, 1], F32, name="rstd")
-            nc.scalar.activation(
-                out=rstd2[:], in_=sum_squares[:], func=ACT.Abs_reciprocal_sqrt,
-                scale=1.0 / (D * D * D), bias=EPS_LN,
-            )
-            normed[i] = (z_i, z_sum_i, rstd2)
-        for i in (2, 3):
-            z_i, z_sum_i, rstd2 = normed[i]
-            neg_mean = per_tile.tile([P, 1], F32, name="neg_mean")
-            nc.vector.tensor_scalar_mul(out=neg_mean[:], in0=z_sum_i[:], scalar1=-1.0 / D)
-            normed[i] = (z_i, neg_mean, rstd2)
-        for i in range(1, TILES):
-            vector_normalise_and_store(i, *normed[i])
+        quantise(0)
+        multiply(0)
+        transpose_tile(1)
+        transpose_tile(2)
+        stats0 = vector_stats(0)
+        copy_tile(1)
+        copy_tile(2)
+        vector_aggregate(0, stats0)
+        quantise(1)
+        multiply(1)
+        centre_and_gain(0)
+        transpose_tile(3)
+        copy_tile(3)
+        quantise(2)
+        fold(2)
+        multiply(2)
+        scalar_sum(2)
+        scalar_first_squares(2)
+        stats1 = vector_stats(1)
+        add_residual(0)
+        quantise(3)
+        fold(3)
+        multiply(3)
+        vector_aggregate(1, stats1)
+        scalar_first_rstd(2)
+        scalar_sum(3)
+        scalar_first_squares(3)
+        scalar_first_rstd(3)
+        second_squares(0)
+        second_mean(0, nc.scalar.mul)
+        second_rstd(0)
+        centre_and_gain(1)
+        centre_and_gain(2)
+        add_residual(1)
+        second_squares(1)
+        second_mean(1, nc.scalar.mul)
+        second_rstd(1)
+        centre_and_gain(3)
+        add_residual(2)
+        second_squares(2)
+        second_rstd(2)
+        normalise_and_store(0)
+        add_residual(3)
+        second_squares(3)
+        second_rstd(3)
+        second_mean(2, nc.vector.tensor_scalar_mul)
+        normalise_and_store(1)
+        second_mean(3, nc.vector.tensor_scalar_mul)
+        for i in range(2, TILES):
+            normalise_and_store(i)

@@ -52,6 +52,15 @@ def tile_bdhlayer_pc_s_kernel(
             out=activity_cols[:], in_=running_activity.rearrange("(p c) -> p c", c=vec_chunks)
         )
         nc.scalar.dma_start(out=scale_cols[:], in_=scale.rearrange("(p c) -> p c", c=vec_chunks))
+        zeros = const.tile([P, P], F32)
+        nc.vector.memset(zeros[:], 0.0)
+        idle_ps = psum_fold.tile([P, FOLD], F32, name="quarters")
+
+        def keep_tensor_busy():
+            nc.tensor.matmul(idle_ps[:], zeros[:], zeros[:], start=True, stop=True)
+
+        for c in range(3):
+            keep_tensor_busy()
         w_scales = const.tile([P, D], U8, align_bytes=64)
         nc.vector.memset(w_scales[:].bitcast(I32), 0)
 
@@ -81,7 +90,7 @@ def tile_bdhlayer_pc_s_kernel(
         nc.scalar.activation(out=table_warm[:], in_=one[:], func=ACT.Abs_reciprocal_sqrt)
 
         xt, grouped, codes, quarters, y_ps = {}, {}, {}, {}, {}
-        mean, rstd, centred, z, z_sum = {}, {}, {}, {}, {}
+        mean, variance, rstd, centred, z, z_sum = {}, {}, {}, {}, {}, {}
         neg_mean, sum_squares, sum_squares2, neg_mean2, rstd2 = {}, {}, {}, {}, {}
 
         def column(name):
@@ -141,10 +150,12 @@ def tile_bdhlayer_pc_s_kernel(
         def vector_aggregate(i, stats):
             mean_var = per_tile.tile([P, 2], F32, name="mean_var")
             nc.vector.bn_aggr(out=mean_var[:], in_=stats[:])
-            mean[i] = mean_var[:, 0:1]
+            mean[i], variance[i] = mean_var[:, 0:1], mean_var[:, 1:2]
+
+        def first_rstd(i):
             rstd[i] = column("rstd1")
             nc.scalar.activation(
-                out=rstd[i][:], in_=mean_var[:, 1:2], func=ACT.Abs_reciprocal_sqrt, bias=EPS_LN
+                out=rstd[i][:], in_=variance[i], func=ACT.Abs_reciprocal_sqrt, bias=EPS_LN
             )
 
         def scalar_sum(i):
@@ -201,9 +212,9 @@ def tile_bdhlayer_pc_s_kernel(
                 bias=EPS_LN,
             )
 
-        def second_mean(i, engine_mul):
+        def second_mean(i):
             neg_mean2[i] = column("neg_mean2")
-            engine_mul(neg_mean2[i][:], z_sum[i][:], -1.0 / D)
+            nc.vector.tensor_scalar_mul(out=neg_mean2[i][:], in0=z_sum[i][:], scalar1=-1.0 / D)
 
         def centre_and_gain(i):
             centred[i] = per_tile.tile([P, D], F32, name="centred")
@@ -267,6 +278,7 @@ def tile_bdhlayer_pc_s_kernel(
                 gain_cols[:, c : c + 1].to_broadcast([P, P]),
                 ident_f32[:],
             )
+        keep_tensor_busy()
         gain = const.tile([P, D], F32)
         nc.scalar.copy(
             out=gain[:].rearrange("p (n c) -> p n c", c=vec_chunks),
@@ -276,11 +288,13 @@ def tile_bdhlayer_pc_s_kernel(
         quantise(0)
         multiply(0)
         transpose_tile(1)
-        transpose_tile(2)
-        stats0 = vector_stats(0)
         copy_tile(1)
+        transpose_tile(2)
         copy_tile(2)
+        keep_tensor_busy()
+        stats0 = vector_stats(0)
         vector_aggregate(0, stats0)
+        first_rstd(0)
         quantise(1)
         multiply(1)
         centre_and_gain(0)
@@ -297,29 +311,30 @@ def tile_bdhlayer_pc_s_kernel(
         fold(3)
         multiply(3)
         vector_aggregate(1, stats1)
-        scalar_first_rstd(2)
+        first_rstd(1)
+        second_mean(0)
         scalar_sum(3)
+        scalar_first_rstd(2)
         scalar_first_squares(3)
-        scalar_first_rstd(3)
         second_squares(0)
-        second_mean(0, nc.scalar.mul)
-        second_rstd(0)
+        scalar_first_rstd(3)
         centre_and_gain(1)
         centre_and_gain(2)
         add_residual(1)
         second_squares(1)
-        second_mean(1, nc.scalar.mul)
+        second_rstd(0)
         second_rstd(1)
         centre_and_gain(3)
+        second_mean(1)
         add_residual(2)
         second_squares(2)
         second_rstd(2)
-        normalise_and_store(0)
         add_residual(3)
         second_squares(3)
         second_rstd(3)
-        second_mean(2, nc.vector.tensor_scalar_mul)
+        second_mean(2)
+        normalise_and_store(0)
         normalise_and_store(1)
-        second_mean(3, nc.vector.tensor_scalar_mul)
+        second_mean(3)
         for i in range(2, TILES):
             normalise_and_store(i)

@@ -48,10 +48,6 @@ def tile_bdhlayer_pc_s_kernel(
         vec_chunks = D // P
         activity_cols = const.tile([P, vec_chunks], BF16)
         scale_cols = const.tile([P, vec_chunks], BF16)
-        nc.scalar.dma_start(
-            out=activity_cols[:], in_=running_activity.rearrange("(p c) -> p c", c=vec_chunks)
-        )
-        nc.scalar.dma_start(out=scale_cols[:], in_=scale.rearrange("(p c) -> p c", c=vec_chunks))
         zeros = const.tile([P, P], F32)
         nc.vector.memset(zeros[:], 0.0)
         idle_ps = psum_fold.tile([P, FOLD], F32, name="quarters")
@@ -71,6 +67,10 @@ def tile_bdhlayer_pc_s_kernel(
         x_sb = const.tile([P, TILES, D], BF16)
 
         nc.sync.dma_start(out=xy_sb[0][:], in_=xy_tiles[0])
+        nc.sync.dma_start(
+            out=activity_cols[:], in_=running_activity.rearrange("(p c) -> p c", c=vec_chunks)
+        )
+        nc.sync.dma_start(out=scale_cols[:], in_=scale.rearrange("(p c) -> p c", c=vec_chunks))
         nc.sync.dma_start(out=w_words[:].bitcast(I32), in_=decoder_words[0].bitcast(I32))
         for q in range(QUADRANTS):
             nc.sync.dma_start(
@@ -79,8 +79,8 @@ def tile_bdhlayer_pc_s_kernel(
             )
         nc.sync.dma_start(out=xy_sb[1][:], in_=xy_tiles[1])
         nc.sync.dma_start(out=xy_sb[2][:], in_=xy_tiles[2])
-        nc.sync.dma_start(out=x_sb[:].rearrange("p i d -> p (i d)"), in_=x_rows)
         nc.sync.dma_start(out=xy_sb[3][:], in_=xy_tiles[3])
+        nc.sync.dma_start(out=x_sb[:].rearrange("p i d -> p (i d)"), in_=x_rows)
 
         ident_f32 = const.tile([P, P], F32)
         make_identity(nc, ident_f32[:])
@@ -329,11 +329,11 @@ def tile_bdhlayer_pc_s_kernel(
         add_residual(2)
         second_squares(2)
         second_rstd(2)
+        normalise_and_store(0)
         add_residual(3)
         second_squares(3)
         second_rstd(3)
         second_mean(2)
-        normalise_and_store(0)
         normalise_and_store(1)
         second_mean(3)
         for i in range(2, TILES):

@@ -90,8 +90,14 @@ def tile_bdhlayer_pc_s_kernel(
         nc.scalar.activation(out=table_warm[:], in_=one[:], func=ACT.Abs_reciprocal_sqrt)
 
         xt, grouped, codes, quarters, y_ps = {}, {}, {}, {}, {}
-        mean, variance, rstd, centred, z, z_sum = {}, {}, {}, {}, {}, {}
-        neg_mean, sum_squares, sum_squares2, neg_mean2, rstd2 = {}, {}, {}, {}, {}
+        mean, variance, centred, z = {}, {}, {}, {}
+        neg_mean = {}
+        sum_squares = const.tile([P, TILES], F32)
+        rstd1 = const.tile([P, TILES], F32)
+        z_sum = const.tile([P, TILES], F32)
+        neg_mean2 = const.tile([P, TILES], F32)
+        sum_squares2 = const.tile([P, TILES], F32)
+        rstd2 = const.tile([P, TILES], F32)
 
         def column(name):
             return per_tile.tile([P, 1], F32, name=name)
@@ -152,10 +158,9 @@ def tile_bdhlayer_pc_s_kernel(
             nc.vector.bn_aggr(out=mean_var[:], in_=stats[:])
             mean[i], variance[i] = mean_var[:, 0:1], mean_var[:, 1:2]
 
-        def first_rstd(i):
-            rstd[i] = column("rstd1")
+        def first_rstd_of_variance(i):
             nc.scalar.activation(
-                out=rstd[i][:], in_=variance[i], func=ACT.Abs_reciprocal_sqrt, bias=EPS_LN
+                out=rstd1[:, i : i + 1], in_=variance[i], func=ACT.Abs_reciprocal_sqrt, bias=EPS_LN
             )
 
         def scalar_sum(i):
@@ -171,20 +176,18 @@ def tile_bdhlayer_pc_s_kernel(
 
         def scalar_first_squares(i):
             squares = per_tile.tile([P, D], F32, name="squares")
-            sum_squares[i] = column("sum_squares")
             nc.scalar.activation(
                 out=squares[:],
                 in_=y_ps[i][:],
                 func=ACT.Square,
                 bias=neg_mean[i][:],
-                accum_out=sum_squares[i][:],
+                accum_out=sum_squares[:, i : i + 1],
             )
 
-        def scalar_first_rstd(i):
-            rstd[i] = column("rstd1")
+        def first_rstd(first, last):
             nc.scalar.activation(
-                out=rstd[i][:],
-                in_=sum_squares[i][:],
+                out=rstd1[:, first:last],
+                in_=sum_squares[:, first:last],
                 func=ACT.Abs_reciprocal_sqrt,
                 scale=1.0 / D,
                 bias=EPS_LN,
@@ -192,29 +195,28 @@ def tile_bdhlayer_pc_s_kernel(
 
         def second_squares(i):
             squares = per_tile.tile([P, D], F32, name="squares")
-            sum_squares2[i] = column("sum_squares2")
             nc.scalar.activation(
                 out=squares[:],
                 in_=z[i][:],
                 func=ACT.Square,
                 scale=-1.0 * D,
-                bias=z_sum[i][:],
-                accum_out=sum_squares2[i][:],
+                bias=z_sum[:, i : i + 1],
+                accum_out=sum_squares2[:, i : i + 1],
             )
 
-        def second_rstd(i):
-            rstd2[i] = column("rstd2")
+        def second_rstd(first, last):
             nc.scalar.activation(
-                out=rstd2[i][:],
-                in_=sum_squares2[i][:],
+                out=rstd2[:, first:last],
+                in_=sum_squares2[:, first:last],
                 func=ACT.Abs_reciprocal_sqrt,
                 scale=1.0 / (D * D * D),
                 bias=EPS_LN,
             )
 
-        def second_mean(i):
-            neg_mean2[i] = column("neg_mean2")
-            nc.vector.tensor_scalar_mul(out=neg_mean2[i][:], in0=z_sum[i][:], scalar1=-1.0 / D)
+        def second_mean(first, last):
+            nc.vector.tensor_scalar_mul(
+                out=neg_mean2[:, first:last], in0=z_sum[:, first:last], scalar1=-1.0 / D
+            )
 
         def centre_and_gain(i):
             centred[i] = per_tile.tile([P, D], F32, name="centred")
@@ -229,15 +231,14 @@ def tile_bdhlayer_pc_s_kernel(
 
         def add_residual(i):
             z[i] = per_tile.tile([P, D], F32, name="z")
-            z_sum[i] = column("z_sum")
             nc.vector.scalar_tensor_tensor(
                 out=z[i][:],
                 in0=centred[i][:],
-                scalar=rstd[i][:],
+                scalar=rstd1[:, i : i + 1],
                 in1=x_sb[:, i, :],
                 op0=ALU.mult,
                 op1=ALU.add,
-                accum_out=z_sum[i][:],
+                accum_out=z_sum[:, i : i + 1],
             )
 
         def normalise_and_store(i):
@@ -245,8 +246,8 @@ def tile_bdhlayer_pc_s_kernel(
             nc.vector.tensor_scalar(
                 out=result[:],
                 in0=z[i][:],
-                scalar1=neg_mean2[i][:],
-                scalar2=rstd2[i][:],
+                scalar1=neg_mean2[:, i : i + 1],
+                scalar2=rstd2[:, i : i + 1],
                 op0=ALU.add,
                 op1=ALU.mult,
             )
@@ -293,48 +294,45 @@ def tile_bdhlayer_pc_s_kernel(
         copy_tile(2)
         keep_tensor_busy()
         stats0 = vector_stats(0)
+        transpose_tile(3)
         vector_aggregate(0, stats0)
-        first_rstd(0)
+        first_rstd_of_variance(0)
+        copy_tile(3)
         quantise(1)
         multiply(1)
         centre_and_gain(0)
-        transpose_tile(3)
-        copy_tile(3)
         quantise(2)
         fold(2)
         multiply(2)
         scalar_sum(2)
         scalar_first_squares(2)
         stats1 = vector_stats(1)
-        add_residual(0)
         quantise(3)
         fold(3)
         multiply(3)
-        vector_aggregate(1, stats1)
-        first_rstd(1)
-        second_mean(0)
         scalar_sum(3)
-        scalar_first_rstd(2)
+        vector_aggregate(1, stats1)
+        first_rstd_of_variance(1)
         scalar_first_squares(3)
+        add_residual(0)
         second_squares(0)
-        scalar_first_rstd(3)
+        first_rstd(2, 4)
         centre_and_gain(1)
         centre_and_gain(2)
         add_residual(1)
         second_squares(1)
-        second_rstd(0)
-        second_rstd(1)
+        second_rstd(0, 1)
+        second_rstd(1, 2)
         centre_and_gain(3)
-        second_mean(1)
+        second_mean(0, 2)
         add_residual(2)
         second_squares(2)
-        second_rstd(2)
+        second_rstd(2, 3)
         normalise_and_store(0)
         add_residual(3)
         second_squares(3)
-        second_rstd(3)
-        second_mean(2)
+        second_rstd(3, 4)
         normalise_and_store(1)
-        second_mean(3)
+        second_mean(2, 4)
         for i in range(2, TILES):
             normalise_and_store(i)

import concourse.mybir as mybir
from concourse.masks import make_identity

F32 = mybir.dt.float32
BF16 = mybir.dt.bfloat16
I32 = mybir.dt.int32
U8 = mybir.dt.uint8
U32 = mybir.dt.uint32
FP8X4 = mybir.dt.float8_e4m3fn_x4
FP4X4 = mybir.dt.float4_e2m1fn_x4
ACT = mybir.ActivationFunctionType
ALU = mybir.AluOpType

P = 128
HEADS = 4
HEAD_DIM = 128
K = HEADS * HEAD_DIM
TOKENS = 512
D = 512
TILES = TOKENS // P
WORD_HALVES = 2
FOLD = 128
QUADRANTS = 4
EPS_LN = 1e-5
TARGET_ACTIVITY = 0.1
EPS_ACTIVITY = 1e-6

FLOPS = 2 * TOKENS * K * D


def tile_bdhlayer_pc_s_kernel(
    tc, xy_sparse, decoder_words, decoder_scales, x, scale, running_activity, out
):
    nc = tc.nc

    xy_tiles = xy_sparse[0].rearrange("h (p i) n -> i p h n", i=TILES)
    x_rows = x[0, 0].rearrange("(p i) d -> p (i d)", i=TILES)
    out_tiles = out[0, 0].rearrange("(p i) d -> i p d", i=TILES)

    with tc.tile_pool(name="const", bufs=1) as const, tc.tile_pool(
        name="per_tile", bufs=TILES
    ) as per_tile, tc.psum_pool(name="psum_y", bufs=TILES) as psum_y, tc.psum_pool(
        name="psum_xt", bufs=2
    ) as psum_xt, tc.psum_pool(name="psum_gain", bufs=1) as psum_gain, tc.psum_pool(
        name="psum_fold", bufs=1
    ) as psum_fold, tc.manual_schedule():

        vec_chunks = D // P
        activity_cols = const.tile([P, vec_chunks], BF16)
        scale_cols = const.tile([P, vec_chunks], BF16)
        zeros = const.tile([P, P], F32)
        nc.vector.memset(zeros[:], 0.0)
        idle_ps = psum_fold.tile([P, FOLD], F32, name="quarters")

        def keep_tensor_busy():
            nc.tensor.matmul(idle_ps[:], zeros[:], zeros[:], start=True, stop=True)

        for c in range(3):
            keep_tensor_busy()
        w_scales = const.tile([P, D], U8, align_bytes=64)
        nc.vector.memset(w_scales[:].bitcast(I32), 0)

        xy_sb = []
        for i in range(TILES):
            xy_sb.append(per_tile.tile([P, HEADS, HEAD_DIM], BF16, name="xy_sb"))
        w_words = const.tile([P, 2 * D], U8, align_bytes=64)
        x_sb = const.tile([P, TILES, D], BF16)

        nc.sync.dma_start(out=xy_sb[0][:], in_=xy_tiles[0])
        nc.sync.dma_start(
            out=activity_cols[:], in_=running_activity.rearrange("(p c) -> p c", c=vec_chunks)
        )
        nc.sync.dma_start(out=scale_cols[:], in_=scale.rearrange("(p c) -> p c", c=vec_chunks))
        nc.sync.dma_start(out=w_words[:].bitcast(I32), in_=decoder_words[0].bitcast(I32))
        for q in range(QUADRANTS):
            nc.sync.dma_start(
                out=w_scales[32 * q : 32 * q + 4, :].bitcast(I32),
                in_=decoder_scales[0, 4 * q : 4 * q + 4, :].bitcast(I32),
            )
        nc.sync.dma_start(out=xy_sb[1][:], in_=xy_tiles[1])
        nc.sync.dma_start(out=xy_sb[2][:], in_=xy_tiles[2])
        nc.sync.dma_start(out=xy_sb[3][:], in_=xy_tiles[3])
        nc.sync.dma_start(out=x_sb[:].rearrange("p i d -> p (i d)"), in_=x_rows)

        ident_f32 = const.tile([P, P], F32)
        make_identity(nc, ident_f32[:])
        one = const.tile([P, 1], F32)
        nc.vector.memset(one[:], 1.0)
        table_warm = const.tile([P, 1], F32)
        nc.scalar.activation(out=table_warm[:], in_=one[:], func=ACT.Abs_reciprocal_sqrt)

        xt, grouped, codes, quarters, y_ps = {}, {}, {}, {}, {}
        mean, variance, centred, z = {}, {}, {}, {}
        neg_mean = {}
        sum_squares = const.tile([P, TILES], F32)
        rstd1 = const.tile([P, TILES], F32)
        z_sum = const.tile([P, TILES], F32)
        neg_mean2 = const.tile([P, TILES], F32)
        sum_squares2 = const.tile([P, TILES], F32)
        rstd2 = const.tile([P, TILES], F32)

        def column(name):
            return per_tile.tile([P, 1], F32, name=name)

        def transpose_tile(i):
            words = xy_sb[i][:].rearrange("p h n -> p (h n)").bitcast(F32)
            xt[i] = psum_xt.tile([P, WORD_HALVES, P], F32, name="xt")
            for u in range(WORD_HALVES):
                nc.tensor.transpose(
                    xt[i][:, u, :], words[:, u : K // 2 : WORD_HALVES], ident_f32[:]
                )

        def copy_tile(i):
            grouped[i] = per_tile.tile([P, P, WORD_HALVES], F32, name="grouped", align_bytes=64)
            copy_out = nc.vector.tensor_copy if i == 0 else nc.scalar.copy
            copy_out(out=grouped[i][:], in_=xt[i][:].rearrange("p u m -> p m u"))

        def quantise(i):
            codes[i] = (
                per_tile.tile([P, P], U32, name="codes", align_bytes=64),
                per_tile.tile([P, P], U8, name="code_scales", align_bytes=64),
            )
            nc.vector.quantize_mx(
                out=codes[i][0][:].bitcast(FP8X4),
                scales=codes[i][1][:],
                in_=grouped[i][:].rearrange("p m u -> p (m u)").bitcast(BF16),
            )

        def decode(i, out, first, last, start, stop):
            nc.tensor.matmul_mx(
                out=out,
                lhsT=codes[i][0][:].bitcast(FP8X4),
                lhsT_scale=codes[i][1][:],
                rhs=w_words[:, 2 * first : 2 * last].bitcast(FP4X4),
                rhs_scale=w_scales[:, first:last],
                start=start,
                stop=stop,
            )

        def multiply(i):
            y_ps[i] = psum_y.tile([P, D], F32, name="y")
            decode(i, y_ps[i][:], 0, D, True, True)

        def fold(i):
            quarters[i] = psum_fold.tile([P, FOLD], F32, name="quarters")
            for c in range(D // FOLD):
                decode(
                    i, quarters[i][:], FOLD * c, FOLD * (c + 1), c == 0, c == D // FOLD - 1
                )

        def vector_stats(i):
            stats = per_tile.tile([P, 6], F32, name="stats")
            nc.vector.bn_stats(out=stats[:], in_=y_ps[i][:])
            return stats

        def vector_aggregate(i, stats):
            mean_var = per_tile.tile([P, 2], F32, name="mean_var")
            nc.vector.bn_aggr(out=mean_var[:], in_=stats[:])
            mean[i], variance[i] = mean_var[:, 0:1], mean_var[:, 1:2]

        def first_rstd_of_variance(i):
            nc.scalar.activation(
                out=rstd1[:, i : i + 1], in_=variance[i], func=ACT.Abs_reciprocal_sqrt, bias=EPS_LN
            )

        def scalar_sum(i):
            copied = per_tile.tile([P, FOLD], F32, name="copied")
            neg_mean[i] = column("neg_mean")
            nc.scalar.activation(
                out=copied[:],
                in_=quarters[i][:],
                func=ACT.Identity,
                scale=-1.0 / D,
                accum_out=neg_mean[i][:],
            )

        def scalar_first_squares(i):
            squares = per_tile.tile([P, D], F32, name="squares")
            nc.scalar.activation(
                out=squares[:],
                in_=y_ps[i][:],
                func=ACT.Square,
                bias=neg_mean[i][:],
                accum_out=sum_squares[:, i : i + 1],
            )

        def first_rstd(first, last):
            nc.scalar.activation(
                out=rstd1[:, first:last],
                in_=sum_squares[:, first:last],
                func=ACT.Abs_reciprocal_sqrt,
                scale=1.0 / D,
                bias=EPS_LN,
            )

        def second_squares(i):
            squares = per_tile.tile([P, D], F32, name="squares")
            nc.scalar.activation(
                out=squares[:],
                in_=z[i][:],
                func=ACT.Square,
                scale=-1.0 * D,
                bias=z_sum[:, i : i + 1],
                accum_out=sum_squares2[:, i : i + 1],
            )

        def second_rstd(first, last):
            nc.scalar.activation(
                out=rstd2[:, first:last],
                in_=sum_squares2[:, first:last],
                func=ACT.Abs_reciprocal_sqrt,
                scale=1.0 / (D * D * D),
                bias=EPS_LN,
            )

        def second_mean(first, last):
            nc.vector.tensor_scalar_mul(
                out=neg_mean2[:, first:last], in0=z_sum[:, first:last], scalar1=-1.0 / D
            )

        def centre_and_gain(i):
            centred[i] = per_tile.tile([P, D], F32, name="centred")
            nc.vector.scalar_tensor_tensor(
                out=centred[i][:],
                in0=y_ps[i][:],
                scalar=mean[i] if i in mean else neg_mean[i][:],
                in1=gain[:],
                op0=ALU.subtract if i in mean else ALU.add,
                op1=ALU.mult,
            )

        def add_residual(i):
            z[i] = per_tile.tile([P, D], F32, name="z")
            nc.vector.scalar_tensor_tensor(
                out=z[i][:],
                in0=centred[i][:],
                scalar=rstd1[:, i : i + 1],
                in1=x_sb[:, i, :],
                op0=ALU.mult,
                op1=ALU.add,
                accum_out=z_sum[:, i : i + 1],
            )

        def normalise_and_store(i):
            result = per_tile.tile([P, D], F32, name="result")
            nc.vector.tensor_scalar(
                out=result[:],
                in0=z[i][:],
                scalar1=neg_mean2[:, i : i + 1],
                scalar2=rstd2[:, i : i + 1],
                op0=ALU.add,
                op1=ALU.mult,
            )
            nc.sync.dma_start(out=out_tiles[i], in_=result[:])

        regulation = const.tile([P, vec_chunks], F32)
        nc.scalar.activation(
            out=regulation[:],
            in_=activity_cols[:],
            func=ACT.Abs_reciprocal_sqrt,
            scale=1.0 / TARGET_ACTIVITY,
            bias=EPS_ACTIVITY / TARGET_ACTIVITY,
        )
        gain_cols = const.tile([P, vec_chunks], F32)
        nc.vector.tensor_tensor(
            out=gain_cols[:],
            in0=regulation[:],
            in1=scale_cols[:],
            op=ALU.mult,
        )

        transpose_tile(0)
        copy_tile(0)

        gain_ps = psum_gain.tile([P, vec_chunks, P], F32)
        for c in range(vec_chunks):
            nc.tensor.transpose(
                gain_ps[:, c, :],
                gain_cols[:, c : c + 1].to_broadcast([P, P]),
                ident_f32[:],
            )
        keep_tensor_busy()
        gain = const.tile([P, D], F32)
        nc.scalar.copy(
            out=gain[:].rearrange("p (n c) -> p n c", c=vec_chunks),
            in_=gain_ps[:].rearrange("p c n -> p n c"),
        )

        quantise(0)
        multiply(0)
        transpose_tile(1)
        copy_tile(1)
        transpose_tile(2)
        copy_tile(2)
        keep_tensor_busy()
        stats0 = vector_stats(0)
        transpose_tile(3)
        vector_aggregate(0, stats0)
        first_rstd_of_variance(0)
        copy_tile(3)
        quantise(1)
        multiply(1)
        centre_and_gain(0)
        quantise(2)
        fold(2)
        multiply(2)
        scalar_sum(2)
        scalar_first_squares(2)
        stats1 = vector_stats(1)
        quantise(3)
        fold(3)
        multiply(3)
        scalar_sum(3)
        vector_aggregate(1, stats1)
        first_rstd_of_variance(1)
        scalar_first_squares(3)
        add_residual(0)
        second_squares(0)
        first_rstd(2, 4)
        centre_and_gain(1)
        centre_and_gain(2)
        add_residual(1)
        second_squares(1)
        second_rstd(0, 1)
        second_rstd(1, 2)
        centre_and_gain(3)
        second_mean(0, 2)
        add_residual(2)
        second_squares(2)
        second_rstd(2, 3)
        normalise_and_store(0)
        add_residual(3)
        second_squares(3)
        second_rstd(3, 4)
        normalise_and_store(1)
        second_mean(2, 4)
        for i in range(2, TILES):
            normalise_and_store(i)
